import numpy as np
import ml_dtypes


def mxq(x, axis, fmt="e4m3"):
    dtype, down = {"e4m3": (ml_dtypes.float8_e4m3fn, 7), "e5m2": (ml_dtypes.float8_e5m2, 14)}[fmt]
    v = np.moveaxis(np.asarray(x, np.float32).astype(ml_dtypes.bfloat16).astype(np.float64), axis, -1)
    blocks = v.reshape(v.shape[:-1] + (-1, 32))
    amax = np.abs(blocks).max(-1, keepdims=True)
    byte = np.maximum(np.where(amax > 0, np.frexp(amax)[1] - 1 + 127, 0) - down, 1)
    scale = np.exp2(byte - 127.0)
    codes = (blocks / scale).astype(np.float32).astype(dtype).astype(np.float64)
    return np.moveaxis((codes * scale).reshape(v.shape), -1, axis)


WIDE = False


def mx_kscale(k):
    if not WIDE:
        return np.ones(k)
    levels = np.array([10, -10, 5, -5, 0])
    a = np.random.permutation(np.resize(levels, k // 512 * 4)).reshape(k // 512, 4)
    idx = np.arange(k)
    return np.exp2(a[idx // 512, idx % 128 // 32])


BF16 = ml_dtypes.bfloat16


def bf(x):
    return np.asarray(x, np.float32).astype(BF16)


def f64(x):
    return np.asarray(x).astype(np.float64)


B, N, D_IN, H, D_HEAD, D_EXPAND = 2, 512, 512, 8, 128, 2048
D_Q = D_HEAD * H
D_V = D_IN * H
D_QKV = 2 * D_Q + D_V
EPS = 1e-5


def feature_norm(x, gamma, beta):
    mean = x.mean(axis=1, keepdims=True)
    var = x.var(axis=1, keepdims=True)
    return gamma * (x - mean) / np.sqrt(var + EPS) + beta


def sigmoid(v):
    e = np.exp(-np.abs(v))
    return np.where(v >= 0.0, 1.0, e) / (1.0 + e)


def swish(v):
    return v * sigmoid(v)


def setup_inputs():
    wcol = np.concatenate([np.full(2 * D_Q, 1.9 / np.sqrt(D_HEAD * D_IN)), np.full(D_V, 0.5 / np.sqrt(D_IN))])
    bcol = np.concatenate([np.full(2 * D_Q, 0.03), np.full(D_V, 0.1)])
    s = mx_kscale(D_IN)
    t = s / s.min()
    return {"x": bf(1.5 * np.random.standard_normal((B, N, D_IN)) + 0.5 * np.random.standard_normal((1, 1, D_IN))),
            "pos_enc": bf(np.random.standard_normal((1, N, D_IN)) * t),
            "gamma1": bf((1.0 + 0.1 * np.random.standard_normal((1, 1, D_IN))) * t),
            "beta1": bf(0.1 * np.random.standard_normal((1, 1, D_IN)) * t),
            "W_qkv": bf(np.random.standard_normal((D_IN, D_QKV)) * wcol / t[:, None]),
            "b_qkv": bf(np.random.standard_normal(D_QKV) * bcol)}


def reference(x, pos_enc, gamma1, beta1, W_qkv, b_qkv):
    h = feature_norm(f64(x), f64(gamma1), f64(beta1)) + f64(pos_enc)
    a = swish(h)
    return (mxq(a, 2, "e4m3") @ mxq(f64(W_qkv), 0, "e4m3")) + f64(b_qkv)

@@ -1,0 +1,216 @@
+from contextlib import ExitStack
+
+import concourse.mybir as mybir
+from concourse.masks import make_identity
+
+F32 = mybir.dt.float32
+BF16 = mybir.dt.bfloat16
+U32 = mybir.dt.uint32
+U8 = mybir.dt.uint8
+FP8X4 = mybir.dt.float8_e4m3fn_x4
+ALU = mybir.AluOpType
+ACT = mybir.ActivationFunctionType
+
+P = 128
+PACK = 4
+BATCH, TOKENS, D_IN, D_OUT = 2, 512, 512, 6144
+EPS = 1e-5
+TOKEN_TILES = TOKENS // P
+UNITS = BATCH * TOKEN_TILES
+N_PASS = 512
+PASSES_PER_STORE = 4
+GROUP = N_PASS * PASSES_PER_STORE
+N_GROUPS = D_OUT // GROUP
+UNITS_PER_CHUNK = UNITS // PASSES_PER_STORE
+SCALAR_SHARE = 4
+RUN = 4
+
+FLOPS = 2 * BATCH * TOKENS * D_IN * D_OUT
+
+
+def regroup(copy, grouped, planes):
+    copy(
+        out=grouped.rearrange("p (c i) t -> p c t i", i=RUN),
+        in_=planes.rearrange("p t (c i) -> p c t i", i=RUN),
+    )
+
+
+def tile_attentionblock_pa_kernel(tc, x, pos_enc, gamma1, beta1, W_qkv, b_qkv, out):
+    nc = tc.nc
+    with ExitStack() as ctx:
+        ctx.enter_context(tc.manual_schedule())
+        keep = ctx.enter_context(tc.tile_pool(name="keep", bufs=1))
+        w_stage = ctx.enter_context(tc.tile_pool(name="w_stage", bufs=4))
+        out_stage = ctx.enter_context(tc.tile_pool(name="out_stage", bufs=6))
+
+        ident = keep.tile([P, P], BF16)
+        make_identity(nc, ident[:])
+        one = keep.tile([P, 1], F32)
+        nc.vector.memset(one[:], 1.0)
+        warm = keep.tile([P, 2], F32)
+        gain_rows = keep.tile([P, P], BF16)
+        nc.vector.memset(gain_rows[:], 0.0)
+
+        nc.scalar.dma_start(out=gain_rows[0:PACK, :], in_=gamma1.rearrange("a b (t p) -> (a b t) p", p=P))
+        nc.scalar.dma_start(out=gain_rows[PACK : 2 * PACK, :], in_=beta1.rearrange("a b (t p) -> (a b t) p", p=P))
+        nc.scalar.activation(out=warm[:, 0:1], in_=one[:], func=ACT.Sqrt)
+
+        x_sb = [keep.tile([P, TOKEN_TILES, D_IN], BF16, name="x_sb%d" % b) for b in range(BATCH)]
+        pos_sb = keep.tile([P, TOKEN_TILES, D_IN], BF16)
+        w_raw = [keep.tile([P, PACK, GROUP], BF16, name="w_raw%d" % g) for g in range(N_GROUPS)]
+        bias_sb = keep.tile([P, D_OUT], BF16)
+        w_planes = W_qkv.rearrange("(t p) n -> p t n", p=P)
+        for b in range(BATCH):
+            nc.sync.dma_start(out=x_sb[b][:], in_=x[b].rearrange("(m i) d -> m i d", i=TOKEN_TILES))
+        nc.sync.dma_start(out=pos_sb[:], in_=pos_enc[0].rearrange("(m i) d -> m i d", i=TOKEN_TILES))
+        nc.sync.dma_start(out=w_raw[0][:], in_=w_planes[:, :, 0:GROUP])
+        nc.sync.dma_start(out=bias_sb[:], in_=b_qkv.partition_broadcast(P))
+        for g in range(1, N_GROUPS):
+            nc.sync.dma_start(out=w_raw[g][:], in_=w_planes[:, :, g * GROUP : (g + 1) * GROUP])
+
+        w_codes = keep.tile([P, D_OUT], U32, align_bytes=64)
+        w_scales = keep.tile([P, D_OUT], U8, align_bytes=64)
+        w_grouped = {}
+
+        def regroup_w_chunk(c, copy):
+            g, j = divmod(c, PASSES_PER_STORE)
+            w_grouped[c] = w_stage.tile([P, N_PASS, PACK], BF16, name="w_grouped", align_bytes=64)
+            regroup(copy, w_grouped[c][:], w_raw[g][:, :, j * N_PASS : (j + 1) * N_PASS])
+
+        def quantise_w_chunk(c):
+            cols = slice(c * N_PASS, (c + 1) * N_PASS)
+            nc.vector.quantize_mx(
+                out=w_codes[:, cols].bitcast(FP8X4),
+                scales=w_scales[:, cols],
+                in_=w_grouped[c][:].rearrange("p n t -> p (n t)"),
+            )
+
+        stats = keep.tile([P, BATCH * PACK, 6], F32)
+        mean_var = keep.tile([P, BATCH * PACK, 2], F32)
+        gains = keep.tile([P, 2 * PACK], F32)
+        posT_sb = keep.tile([P, PACK, TOKENS], BF16)
+        a_planes = [keep.tile([P, PACK, TOKENS], BF16, name="a_planes%d" % b) for b in range(BATCH)]
+        a_grouped = [keep.tile([P, TOKENS, PACK], BF16, name="a_grouped%d" % b, align_bytes=64) for b in range(BATCH)]
+        a_codes = [keep.tile([P, TOKENS], U32, name="a_codes%d" % b, align_bytes=64) for b in range(BATCH)]
+        a_scales = [keep.tile([P, TOKENS], U8, name="a_scales%d" % b, align_bytes=64) for b in range(BATCH)]
+
+        with tc.psum_pool(name="head_psum", bufs=1) as head_psum:
+
+            def transpose_planes(rows_sb, name):
+                banks = []
+                for h in range(PACK // 2):
+                    bank = head_psum.tile([P, 2, TOKENS], BF16, name="%s_%d" % (name, h))
+                    for t2 in range(2):
+                        t = 2 * h + t2
+                        for i in range(TOKEN_TILES):
+                            nc.tensor.transpose(
+                                bank[:, t2, i * P : (i + 1) * P], rows_sb[:, i, t * P : (t + 1) * P], ident[:]
+                            )
+                    banks.append(bank)
+                return banks
+
+            xT = []
+            for b in range(BATCH):
+                xT.append(transpose_planes(x_sb[b], "xT%d" % b))
+                for t in range(PACK):
+                    nc.vector.bn_stats(out=stats[:, b * PACK + t, :], in_=xT[b][t // 2][:, t % 2, :])
+                for t in range(PACK):
+                    nc.vector.bn_aggr(out=mean_var[:, b * PACK + t, :], in_=stats[:, b * PACK + t, :])
+
+            gainsT = head_psum.tile([P, P], BF16)
+            nc.tensor.transpose(gainsT[:], gain_rows[:], ident[:])
+            nc.vector.tensor_copy(out=gains[:], in_=gainsT[:, 0 : 2 * PACK])
+            posT = transpose_planes(pos_sb, "posT")
+
+            std = keep.tile([P, BATCH, PACK], F32)
+            rstd = keep.tile([P, BATCH, PACK], F32)
+            scale = keep.tile([P, BATCH, PACK], F32)
+            mean_scale = keep.tile([P, BATCH, PACK], F32)
+            shift = keep.tile([P, BATCH, PACK], F32)
+            mean = mean_var[:, :, 0].rearrange("p (b t) -> p b t", b=BATCH)
+            var = mean_var[:, :, 1].rearrange("p (b t) -> p b t", b=BATCH)
+            gamma = gains[:, 0:PACK].unsqueeze(1).to_broadcast([P, BATCH, PACK])
+            beta = gains[:, PACK : 2 * PACK].unsqueeze(1).to_broadcast([P, BATCH, PACK])
+            nc.scalar.copy(out=posT_sb[:, 0:2, :], in_=posT[0][:])
+            nc.scalar.activation(out=std[:], in_=var, func=ACT.Sqrt, bias=EPS, scale=1.0)
+            nc.scalar.activation(out=warm[:, 1:2], in_=std[:, 0, 0:1], func=ACT.Silu)
+            nc.scalar.copy(out=posT_sb[:, 2:4, :], in_=posT[1][:])
+            nc.vector.reciprocal(out=rstd[:], in_=std[:])
+            nc.vector.tensor_tensor(out=scale[:], in0=rstd[:], in1=gamma, op=ALU.mult)
+            nc.vector.tensor_tensor(out=mean_scale[:], in0=mean, in1=scale[:], op=ALU.mult)
+            nc.vector.tensor_tensor(out=shift[:], in0=beta, in1=mean_scale[:], op=ALU.subtract)
+
+            for b in range(BATCH):
+                h_planes = keep.tile([P, PACK, TOKENS], F32, name="h_planes%d" % b)
+                for t in range(PACK):
+                    nc.vector.scalar_tensor_tensor(
+                        out=h_planes[:, t, :],
+                        in0=xT[b][t // 2][:, t % 2, :],
+                        scalar=scale[:, b, t : t + 1],
+                        in1=posT_sb[:, t, :],
+                        op0=ALU.mult,
+                        op1=ALU.add,
+                    )
+                    nc.scalar.activation(
+                        out=a_planes[b][:, t, :],
+                        in_=h_planes[:, t, :],
+                        func=ACT.Silu,
+                        bias=shift[:, b, t : t + 1],
+                        scale=1.0,
+                    )
+
+        def quantise_a(b):
+            nc.vector.quantize_mx(
+                out=a_codes[b][:].bitcast(FP8X4),
+                scales=a_scales[b][:],
+                in_=a_grouped[b][:].rearrange("p n t -> p (n t)"),
+            )
+
+        half = PASSES_PER_STORE // 2
+        for c in range(half):
+            regroup_w_chunk(c, nc.vector.tensor_copy)
+        for c in range(half, PASSES_PER_STORE):
+            regroup_w_chunk(c, nc.scalar.copy)
+        regroup(nc.vector.tensor_copy, a_grouped[0][:], a_planes[0][:])
+        for c in range(half):
+            quantise_w_chunk(c)
+        regroup(nc.vector.tensor_copy, a_grouped[1][:], a_planes[1][:])
+        quantise_a(0)
+        quantise_a(1)
+        for c in range(half, PASSES_PER_STORE):
+            quantise_w_chunk(c)
+
+        acc_psum = ctx.enter_context(tc.psum_pool(name="acc_psum", bufs=8, reuse_waits="tile"))
+        for g in range(N_GROUPS):
+            for u in range(UNITS):
+                b, i = divmod(u, TOKEN_TILES)
+                tokens = slice(i * P, (i + 1) * P)
+                result = out_stage.tile([P, GROUP], F32)
+                for j in range(PASSES_PER_STORE):
+                    cols = slice(g * GROUP + j * N_PASS, g * GROUP + (j + 1) * N_PASS)
+                    acc = acc_psum.tile([P, N_PASS], F32)
+                    nc.tensor.matmul_mx(
+                        out=acc[:],
+                        lhsT=a_codes[b][:, tokens].bitcast(FP8X4),
+                        lhsT_scale=a_scales[b][:, tokens],
+                        rhs=w_codes[:, cols].bitcast(FP8X4),
+                        rhs_scale=w_scales[:, cols],
+                        start=True,
+                        stop=True,
+                    )
+                    part = result[:, j * N_PASS : (j + 1) * N_PASS]
+                    if (u * PASSES_PER_STORE + j) % SCALAR_SHARE < SCALAR_SHARE - 1:
+                        nc.vector.tensor_tensor(out=part, in0=acc[:], in1=bias_sb[:, cols], op=ALU.add)
+                    else:
+                        nc.scalar.copy(out=part, in_=acc[:])
+                        nc.gpsimd.tensor_tensor(out=part, in0=part, in1=bias_sb[:, cols], op=ALU.add)
+                nc.sync.dma_start(
+                    out=out[b].rearrange("(m i) n -> i m n", i=TOKEN_TILES)[i, :, g * GROUP : (g + 1) * GROUP],
+                    in_=result[:],
+                )
+                if g + 1 < N_GROUPS:
+                    c = (g + 1) * PASSES_PER_STORE + u // UNITS_PER_CHUNK
+                    if u % UNITS_PER_CHUNK == 0:
+                        regroup_w_chunk(c, nc.scalar.copy)
+                    if u % UNITS_PER_CHUNK == 1:
+                        quantise_w_chunk(c)

@@ -18,11 +18,11 @@ EPS = 1e-5
 TOKEN_TILES = TOKENS // P
 UNITS = BATCH * TOKEN_TILES
 N_PASS = 512
-PASSES_PER_STORE = 4
+HALF = N_PASS // 2
+PASSES_PER_STORE = 3
 GROUP = N_PASS * PASSES_PER_STORE
 N_GROUPS = D_OUT // GROUP
-UNITS_PER_CHUNK = UNITS // PASSES_PER_STORE
-SCALAR_SHARE = 4
+BANK_BF16 = 1024
 RUN = 4
 
 FLOPS = 2 * BATCH * TOKENS * D_IN * D_OUT
@@ -41,20 +41,19 @@ def tile_attentionblock_pa_kernel(tc, x, pos_enc, gamma1, beta1, W_qkv, b_qkv, o
         ctx.enter_context(tc.manual_schedule())
         keep = ctx.enter_context(tc.tile_pool(name="keep", bufs=1))
         w_stage = ctx.enter_context(tc.tile_pool(name="w_stage", bufs=4))
-        out_stage = ctx.enter_context(tc.tile_pool(name="out_stage", bufs=6))
+        out_stage = ctx.enter_context(tc.tile_pool(name="out_stage", bufs=8))
 
-        ident = keep.tile([P, P], BF16)
-        make_identity(nc, ident[:])
-        one = keep.tile([P, 1], F32)
-        nc.vector.memset(one[:], 1.0)
-        warm = keep.tile([P, 2], F32)
         gain_rows = keep.tile([P, P], BF16)
         nc.vector.memset(gain_rows[:], 0.0)
-
-        nc.scalar.dma_start(out=gain_rows[0:PACK, :], in_=gamma1.rearrange("a b (t p) -> (a b t) p", p=P))
-        nc.scalar.dma_start(out=gain_rows[PACK : 2 * PACK, :], in_=beta1.rearrange("a b (t p) -> (a b t) p", p=P))
+        one = keep.tile([P, 1], F32)
+        nc.vector.memset(one[:], 1.0)
+        ident = keep.tile([P, P], BF16)
+        make_identity(nc, ident[:])
+        warm = keep.tile([P, 2], F32)
         nc.scalar.activation(out=warm[:, 0:1], in_=one[:], func=ACT.Sqrt)
 
+        nc.sync.dma_start(out=gain_rows[0:PACK, :], in_=gamma1.rearrange("a b (t p) -> (a b t) p", p=P))
+        nc.sync.dma_start(out=gain_rows[PACK : 2 * PACK, :], in_=beta1.rearrange("a b (t p) -> (a b t) p", p=P))
         x_sb = [keep.tile([P, TOKEN_TILES, D_IN], BF16, name="x_sb%d" % b) for b in range(BATCH)]
         pos_sb = keep.tile([P, TOKEN_TILES, D_IN], BF16)
         w_raw = [keep.tile([P, PACK, GROUP], BF16, name="w_raw%d" % g) for g in range(N_GROUPS)]
@@ -68,14 +67,96 @@ def tile_attentionblock_pa_kernel(tc, x, pos_enc, gamma1, beta1, W_qkv, b_qkv, o
         for g in range(1, N_GROUPS):
             nc.sync.dma_start(out=w_raw[g][:], in_=w_planes[:, :, g * GROUP : (g + 1) * GROUP])
 
+        xT = [keep.tile([P, PACK, TOKENS], BF16, name="xT%d" % b) for b in range(BATCH)]
+        posT = keep.tile([P, PACK, TOKENS], BF16)
+        gains = keep.tile([P, 2 * PACK], F32)
+        stats = keep.tile([P, BATCH * PACK, 6], F32)
+        mean_var = keep.tile([P, BATCH * PACK, 2], F32)
+
+        with tc.psum_pool(name="head_psum", bufs=8) as head_psum:
+            bank = head_psum.tile([P, BANK_BF16], BF16, name="bank")
+            nc.tensor.transpose(bank[:, 0:P], gain_rows[:], ident[:])
+            nc.vector.tensor_copy(out=gains[:], in_=bank[:, 0 : 2 * PACK])
+
+            def transpose_plane(rows_sb, t, plane):
+                bank = head_psum.tile([P, BANK_BF16], BF16, name="bank")
+                for i in range(TOKEN_TILES):
+                    nc.tensor.transpose(bank[:, i * P : (i + 1) * P], rows_sb[:, i, t * P : (t + 1) * P], ident[:])
+                nc.scalar.copy(out=plane, in_=bank[:, 0:TOKENS])
+
+            for b in range(BATCH):
+                for t in range(PACK):
+                    transpose_plane(x_sb[b], t, xT[b][:, t, :])
+                    nc.vector.bn_stats(out=stats[:, b * PACK + t, :], in_=xT[b][:, t, :])
+                for t in range(PACK):
+                    nc.vector.bn_aggr(out=mean_var[:, b * PACK + t, :], in_=stats[:, b * PACK + t, :])
+            for t in range(PACK):
+                transpose_plane(pos_sb, t, posT[:, t, :])
+
+        std = keep.tile([P, BATCH, PACK], F32)
+        rstd = keep.tile([P, BATCH, PACK], F32)
+        scale = keep.tile([P, BATCH, PACK], F32)
+        mean_scale = keep.tile([P, BATCH, PACK], F32)
+        shift = keep.tile([P, BATCH, PACK], F32)
+        mean = mean_var[:, :, 0].rearrange("p (b t) -> p b t", b=BATCH)
+        var = mean_var[:, :, 1].rearrange("p (b t) -> p b t", b=BATCH)
+        gamma = gains[:, 0:PACK].unsqueeze(1).to_broadcast([P, BATCH, PACK])
+        beta = gains[:, PACK : 2 * PACK].unsqueeze(1).to_broadcast([P, BATCH, PACK])
+        nc.scalar.activation(out=std[:], in_=var, func=ACT.Sqrt, bias=EPS, scale=1.0)
+        nc.scalar.activation(out=warm[:, 1:2], in_=std[:, 0, 0:1], func=ACT.Silu)
+        nc.vector.reciprocal(out=rstd[:], in_=std[:])
+        nc.vector.tensor_tensor(out=scale[:], in0=rstd[:], in1=gamma, op=ALU.mult)
+        nc.vector.tensor_tensor(out=mean_scale[:], in0=mean, in1=scale[:], op=ALU.mult)
+        nc.vector.tensor_tensor(out=shift[:], in0=beta, in1=mean_scale[:], op=ALU.subtract)
+
+        h_planes = [keep.tile([P, PACK, TOKENS], F32, name="h_planes%d" % b) for b in range(BATCH)]
+        a_planes = [keep.tile([P, PACK, TOKENS], BF16, name="a_planes%d" % b) for b in range(BATCH)]
+        a_grouped = [keep.tile([P, TOKENS, PACK], BF16, name="a_grouped%d" % b, align_bytes=64) for b in range(BATCH)]
+        a_codes = [keep.tile([P, TOKENS], U32, name="a_codes%d" % b, align_bytes=64) for b in range(BATCH)]
+        a_scales = [keep.tile([P, TOKENS], U8, name="a_scales%d" % b, align_bytes=64) for b in range(BATCH)]
+
+        def swish(b):
+            for t in range(PACK):
+                nc.vector.scalar_tensor_tensor(
+                    out=h_planes[b][:, t, :],
+                    in0=xT[b][:, t, :],
+                    scalar=scale[:, b, t : t + 1],
+                    in1=posT[:, t, :],
+                    op0=ALU.mult,
+                    op1=ALU.add,
+                )
+                nc.scalar.activation(
+                    out=a_planes[b][:, t, :],
+                    in_=h_planes[b][:, t, :],
+                    func=ACT.Silu,
+                    bias=shift[:, b, t : t + 1],
+                    scale=1.0,
+                )
+
+        def regroup_a(b):
+            regroup(nc.vector.tensor_copy, a_grouped[b][:], a_planes[b][:])
+
+        def quantise_a(b):
+            nc.vector.quantize_mx(
+                out=a_codes[b][:].bitcast(FP8X4),
+                scales=a_scales[b][:],
+                in_=a_grouped[b][:].rearrange("p n t -> p (n t)"),
+            )
+
         w_codes = keep.tile([P, D_OUT], U32, align_bytes=64)
         w_scales = keep.tile([P, D_OUT], U8, align_bytes=64)
         w_grouped = {}
 
-        def regroup_w_chunk(c, copy):
+        def regroup_w_half(c, half, copy):
             g, j = divmod(c, PASSES_PER_STORE)
-            w_grouped[c] = w_stage.tile([P, N_PASS, PACK], BF16, name="w_grouped", align_bytes=64)
-            regroup(copy, w_grouped[c][:], w_raw[g][:, :, j * N_PASS : (j + 1) * N_PASS])
+            if half == 0:
+                w_grouped[c] = w_stage.tile([P, N_PASS, PACK], BF16, name="w_grouped", align_bytes=64)
+            first = half * HALF
+            regroup(
+                copy,
+                w_grouped[c][:, first : first + HALF, :],
+                w_raw[g][:, :, j * N_PASS + first : j * N_PASS + first + HALF],
+            )
 
         def quantise_w_chunk(c):
             cols = slice(c * N_PASS, (c + 1) * N_PASS)
@@ -85,105 +166,26 @@ def tile_attentionblock_pa_kernel(tc, x, pos_enc, gamma1, beta1, W_qkv, b_qkv, o
                 in_=w_grouped[c][:].rearrange("p n t -> p (n t)"),
             )
 
-        stats = keep.tile([P, BATCH * PACK, 6], F32)
-        mean_var = keep.tile([P, BATCH * PACK, 2], F32)
-        gains = keep.tile([P, 2 * PACK], F32)
-        posT_sb = keep.tile([P, PACK, TOKENS], BF16)
-        a_planes = [keep.tile([P, PACK, TOKENS], BF16, name="a_planes%d" % b) for b in range(BATCH)]
-        a_grouped = [keep.tile([P, TOKENS, PACK], BF16, name="a_grouped%d" % b, align_bytes=64) for b in range(BATCH)]
-        a_codes = [keep.tile([P, TOKENS], U32, name="a_codes%d" % b, align_bytes=64) for b in range(BATCH)]
-        a_scales = [keep.tile([P, TOKENS], U8, name="a_scales%d" % b, align_bytes=64) for b in range(BATCH)]
-
-        with tc.psum_pool(name="head_psum", bufs=1) as head_psum:
-
-            def transpose_planes(rows_sb, name):
-                banks = []
-                for h in range(PACK // 2):
-                    bank = head_psum.tile([P, 2, TOKENS], BF16, name="%s_%d" % (name, h))
-                    for t2 in range(2):
-                        t = 2 * h + t2
-                        for i in range(TOKEN_TILES):
-                            nc.tensor.transpose(
-                                bank[:, t2, i * P : (i + 1) * P], rows_sb[:, i, t * P : (t + 1) * P], ident[:]
-                            )
-                    banks.append(bank)
-                return banks
-
-            xT = []
-            for b in range(BATCH):
-                xT.append(transpose_planes(x_sb[b], "xT%d" % b))
-                for t in range(PACK):
-                    nc.vector.bn_stats(out=stats[:, b * PACK + t, :], in_=xT[b][t // 2][:, t % 2, :])
-                for t in range(PACK):
-                    nc.vector.bn_aggr(out=mean_var[:, b * PACK + t, :], in_=stats[:, b * PACK + t, :])
-
-            gainsT = head_psum.tile([P, P], BF16)
-            nc.tensor.transpose(gainsT[:], gain_rows[:], ident[:])
-            nc.vector.tensor_copy(out=gains[:], in_=gainsT[:, 0 : 2 * PACK])
-            posT = transpose_planes(pos_sb, "posT")
-
-            std = keep.tile([P, BATCH, PACK], F32)
-            rstd = keep.tile([P, BATCH, PACK], F32)
-            scale = keep.tile([P, BATCH, PACK], F32)
-            mean_scale = keep.tile([P, BATCH, PACK], F32)
-            shift = keep.tile([P, BATCH, PACK], F32)
-            mean = mean_var[:, :, 0].rearrange("p (b t) -> p b t", b=BATCH)
-            var = mean_var[:, :, 1].rearrange("p (b t) -> p b t", b=BATCH)
-            gamma = gains[:, 0:PACK].unsqueeze(1).to_broadcast([P, BATCH, PACK])
-            beta = gains[:, PACK : 2 * PACK].unsqueeze(1).to_broadcast([P, BATCH, PACK])
-            nc.scalar.copy(out=posT_sb[:, 0:2, :], in_=posT[0][:])
-            nc.scalar.activation(out=std[:], in_=var, func=ACT.Sqrt, bias=EPS, scale=1.0)
-            nc.scalar.activation(out=warm[:, 1:2], in_=std[:, 0, 0:1], func=ACT.Silu)
-            nc.scalar.copy(out=posT_sb[:, 2:4, :], in_=posT[1][:])
-            nc.vector.reciprocal(out=rstd[:], in_=std[:])
-            nc.vector.tensor_tensor(out=scale[:], in0=rstd[:], in1=gamma, op=ALU.mult)
-            nc.vector.tensor_tensor(out=mean_scale[:], in0=mean, in1=scale[:], op=ALU.mult)
-            nc.vector.tensor_tensor(out=shift[:], in0=beta, in1=mean_scale[:], op=ALU.subtract)
-
-            for b in range(BATCH):
-                h_planes = keep.tile([P, PACK, TOKENS], F32, name="h_planes%d" % b)
-                for t in range(PACK):
-                    nc.vector.scalar_tensor_tensor(
-                        out=h_planes[:, t, :],
-                        in0=xT[b][t // 2][:, t % 2, :],
-                        scalar=scale[:, b, t : t + 1],
-                        in1=posT_sb[:, t, :],
-                        op0=ALU.mult,
-                        op1=ALU.add,
-                    )
-                    nc.scalar.activation(
-                        out=a_planes[b][:, t, :],
-                        in_=h_planes[:, t, :],
-                        func=ACT.Silu,
-                        bias=shift[:, b, t : t + 1],
-                        scale=1.0,
-                    )
-
-        def quantise_a(b):
-            nc.vector.quantize_mx(
-                out=a_codes[b][:].bitcast(FP8X4),
-                scales=a_scales[b][:],
-                in_=a_grouped[b][:].rearrange("p n t -> p (n t)"),
-            )
-
-        half = PASSES_PER_STORE // 2
-        for c in range(half):
-            regroup_w_chunk(c, nc.vector.tensor_copy)
-        for c in range(half, PASSES_PER_STORE):
-            regroup_w_chunk(c, nc.scalar.copy)
-        regroup(nc.vector.tensor_copy, a_grouped[0][:], a_planes[0][:])
-        for c in range(half):
-            quantise_w_chunk(c)
-        regroup(nc.vector.tensor_copy, a_grouped[1][:], a_planes[1][:])
+        swish(0)
+        for half in range(2):
+            regroup_w_half(0, half, nc.vector.tensor_copy)
+        for c in range(1, PASSES_PER_STORE):
+            for half in range(2):
+                regroup_w_half(c, half, nc.scalar.copy)
+        regroup_a(0)
+        quantise_w_chunk(0)
         quantise_a(0)
-        quantise_a(1)
-        for c in range(half, PASSES_PER_STORE):
+        for c in range(1, PASSES_PER_STORE):
             quantise_w_chunk(c)
 
         acc_psum = ctx.enter_context(tc.psum_pool(name="acc_psum", bufs=8, reuse_waits="tile"))
         for g in range(N_GROUPS):
             for u in range(UNITS):
                 b, i = divmod(u, TOKEN_TILES)
+                if g == 0 and b > 0 and i == 0:
+                    swish(b)
+                    regroup_a(b)
+                    quantise_a(b)
                 tokens = slice(i * P, (i + 1) * P)
                 result = out_stage.tile([P, GROUP], F32)
                 for j in range(PASSES_PER_STORE):
@@ -199,18 +201,18 @@ def tile_attentionblock_pa_kernel(tc, x, pos_enc, gamma1, beta1, W_qkv, b_qkv, o
                         stop=True,
                     )
                     part = result[:, j * N_PASS : (j + 1) * N_PASS]
-                    if (u * PASSES_PER_STORE + j) % SCALAR_SHARE < SCALAR_SHARE - 1:
-                        nc.vector.tensor_tensor(out=part, in0=acc[:], in1=bias_sb[:, cols], op=ALU.add)
-                    else:
+                    if j == 0:
                         nc.scalar.copy(out=part, in_=acc[:])
                         nc.gpsimd.tensor_tensor(out=part, in0=part, in1=bias_sb[:, cols], op=ALU.add)
+                    else:
+                        nc.vector.tensor_tensor(out=part, in0=acc[:], in1=bias_sb[:, cols], op=ALU.add)
                 nc.sync.dma_start(
                     out=out[b].rearrange("(m i) n -> i m n", i=TOKEN_TILES)[i, :, g * GROUP : (g + 1) * GROUP],
                     in_=result[:],
                 )
                 if g + 1 < N_GROUPS:
-                    c = (g + 1) * PASSES_PER_STORE + u // UNITS_PER_CHUNK
-                    if u % UNITS_PER_CHUNK == 0:
-                        regroup_w_chunk(c, nc.scalar.copy)
-                    if u % UNITS_PER_CHUNK == 1:
-                        quantise_w_chunk(c)
+                    next_first = (g + 1) * PASSES_PER_STORE
+                    if u < 2 * PASSES_PER_STORE:
+                        regroup_w_half(next_first + u // 2, u % 2, nc.scalar.copy)
+                    if u >= 2 and u % 2 == 0:
+                        quantise_w_chunk(next_first + u // 2 - 1)

@@ -22,10 +22,12 @@ HALF = N_PASS // 2
 PASSES_PER_STORE = 3
 GROUP = N_PASS * PASSES_PER_STORE
 N_GROUPS = D_OUT // GROUP
-BANK_BF16 = 1024
+SCALAR_SHARE = 3
 RUN = 4
 
 FLOPS = 2 * BATCH * TOKENS * D_IN * D_OUT
+
+assert PACK == TOKEN_TILES
 
 
 def regroup(copy, grouped, planes):
@@ -59,89 +61,20 @@ def tile_attentionblock_pa_kernel(tc, x, pos_enc, gamma1, beta1, W_qkv, b_qkv, o
         w_raw = [keep.tile([P, PACK, GROUP], BF16, name="w_raw%d" % g) for g in range(N_GROUPS)]
         bias_sb = keep.tile([P, D_OUT], BF16)
         w_planes = W_qkv.rearrange("(t p) n -> p t n", p=P)
-        for b in range(BATCH):
+
+        def load_x(b):
             nc.sync.dma_start(out=x_sb[b][:], in_=x[b].rearrange("(m i) d -> m i d", i=TOKEN_TILES))
-        nc.sync.dma_start(out=pos_sb[:], in_=pos_enc[0].rearrange("(m i) d -> m i d", i=TOKEN_TILES))
-        nc.sync.dma_start(out=w_raw[0][:], in_=w_planes[:, :, 0:GROUP])
-        nc.sync.dma_start(out=bias_sb[:], in_=b_qkv.partition_broadcast(P))
-        for g in range(1, N_GROUPS):
+
+        def load_w(g):
             nc.sync.dma_start(out=w_raw[g][:], in_=w_planes[:, :, g * GROUP : (g + 1) * GROUP])
 
-        xT = [keep.tile([P, PACK, TOKENS], BF16, name="xT%d" % b) for b in range(BATCH)]
-        posT = keep.tile([P, PACK, TOKENS], BF16)
-        gains = keep.tile([P, 2 * PACK], F32)
-        stats = keep.tile([P, BATCH * PACK, 6], F32)
-        mean_var = keep.tile([P, BATCH * PACK, 2], F32)
-
-        with tc.psum_pool(name="head_psum", bufs=8) as head_psum:
-            bank = head_psum.tile([P, BANK_BF16], BF16, name="bank")
-            nc.tensor.transpose(bank[:, 0:P], gain_rows[:], ident[:])
-            nc.vector.tensor_copy(out=gains[:], in_=bank[:, 0 : 2 * PACK])
-
-            def transpose_plane(rows_sb, t, plane):
-                bank = head_psum.tile([P, BANK_BF16], BF16, name="bank")
-                for i in range(TOKEN_TILES):
-                    nc.tensor.transpose(bank[:, i * P : (i + 1) * P], rows_sb[:, i, t * P : (t + 1) * P], ident[:])
-                nc.scalar.copy(out=plane, in_=bank[:, 0:TOKENS])
-
-            for b in range(BATCH):
-                for t in range(PACK):
-                    transpose_plane(x_sb[b], t, xT[b][:, t, :])
-                    nc.vector.bn_stats(out=stats[:, b * PACK + t, :], in_=xT[b][:, t, :])
-                for t in range(PACK):
-                    nc.vector.bn_aggr(out=mean_var[:, b * PACK + t, :], in_=stats[:, b * PACK + t, :])
-            for t in range(PACK):
-                transpose_plane(pos_sb, t, posT[:, t, :])
-
-        std = keep.tile([P, BATCH, PACK], F32)
-        rstd = keep.tile([P, BATCH, PACK], F32)
-        scale = keep.tile([P, BATCH, PACK], F32)
-        mean_scale = keep.tile([P, BATCH, PACK], F32)
-        shift = keep.tile([P, BATCH, PACK], F32)
-        mean = mean_var[:, :, 0].rearrange("p (b t) -> p b t", b=BATCH)
-        var = mean_var[:, :, 1].rearrange("p (b t) -> p b t", b=BATCH)
-        gamma = gains[:, 0:PACK].unsqueeze(1).to_broadcast([P, BATCH, PACK])
-        beta = gains[:, PACK : 2 * PACK].unsqueeze(1).to_broadcast([P, BATCH, PACK])
-        nc.scalar.activation(out=std[:], in_=var, func=ACT.Sqrt, bias=EPS, scale=1.0)
-        nc.scalar.activation(out=warm[:, 1:2], in_=std[:, 0, 0:1], func=ACT.Silu)
-        nc.vector.reciprocal(out=rstd[:], in_=std[:])
-        nc.vector.tensor_tensor(out=scale[:], in0=rstd[:], in1=gamma, op=ALU.mult)
-        nc.vector.tensor_tensor(out=mean_scale[:], in0=mean, in1=scale[:], op=ALU.mult)
-        nc.vector.tensor_tensor(out=shift[:], in0=beta, in1=mean_scale[:], op=ALU.subtract)
-
-        h_planes = [keep.tile([P, PACK, TOKENS], F32, name="h_planes%d" % b) for b in range(BATCH)]
-        a_planes = [keep.tile([P, PACK, TOKENS], BF16, name="a_planes%d" % b) for b in range(BATCH)]
-        a_grouped = [keep.tile([P, TOKENS, PACK], BF16, name="a_grouped%d" % b, align_bytes=64) for b in range(BATCH)]
-        a_codes = [keep.tile([P, TOKENS], U32, name="a_codes%d" % b, align_bytes=64) for b in range(BATCH)]
-        a_scales = [keep.tile([P, TOKENS], U8, name="a_scales%d" % b, align_bytes=64) for b in range(BATCH)]
-
-        def swish(b):
-            for t in range(PACK):
-                nc.vector.scalar_tensor_tensor(
-                    out=h_planes[b][:, t, :],
-                    in0=xT[b][:, t, :],
-                    scalar=scale[:, b, t : t + 1],
-                    in1=posT[:, t, :],
-                    op0=ALU.mult,
-                    op1=ALU.add,
-                )
-                nc.scalar.activation(
-                    out=a_planes[b][:, t, :],
-                    in_=h_planes[b][:, t, :],
-                    func=ACT.Silu,
-                    bias=shift[:, b, t : t + 1],
-                    scale=1.0,
-                )
-
-        def regroup_a(b):
-            regroup(nc.vector.tensor_copy, a_grouped[b][:], a_planes[b][:])
-
-        def quantise_a(b):
-            nc.vector.quantize_mx(
-                out=a_codes[b][:].bitcast(FP8X4),
-                scales=a_scales[b][:],
-                in_=a_grouped[b][:].rearrange("p n t -> p (n t)"),
-            )
+        for b in range(BATCH):
+            load_x(b)
+        load_w(0)
+        nc.sync.dma_start(out=pos_sb[:], in_=pos_enc[0].rearrange("(m i) d -> m i d", i=TOKEN_TILES))
+        nc.sync.dma_start(out=bias_sb[:], in_=b_qkv.partition_broadcast(P))
+        for g in range(1, N_GROUPS):
+            load_w(g)
 
         w_codes = keep.tile([P, D_OUT], U32, align_bytes=64)
         w_scales = keep.tile([P, D_OUT], U8, align_bytes=64)
@@ -158,6 +91,9 @@ def tile_attentionblock_pa_kernel(tc, x, pos_enc, gamma1, beta1, W_qkv, b_qkv, o
                 w_raw[g][:, :, j * N_PASS + first : j * N_PASS + first + HALF],
             )
 
+        def gpsimd_copy(out, in_):
+            nc.gpsimd.tensor_scalar(out=out, in0=in_, scalar1=1.0, scalar2=0.0, op0=ALU.mult, op1=ALU.add)
+
         def quantise_w_chunk(c):
             cols = slice(c * N_PASS, (c + 1) * N_PASS)
             nc.vector.quantize_mx(
@@ -166,26 +102,112 @@ def tile_attentionblock_pa_kernel(tc, x, pos_enc, gamma1, beta1, W_qkv, b_qkv, o
                 in_=w_grouped[c][:].rearrange("p n t -> p (n t)"),
             )
 
-        swish(0)
-        for half in range(2):
-            regroup_w_half(0, half, nc.vector.tensor_copy)
-        for c in range(1, PASSES_PER_STORE):
-            for half in range(2):
-                regroup_w_half(c, half, nc.scalar.copy)
-        regroup_a(0)
-        quantise_w_chunk(0)
-        quantise_a(0)
-        for c in range(1, PASSES_PER_STORE):
-            quantise_w_chunk(c)
+        xT = {}
+        posT_sb = keep.tile([P, PACK, TOKENS], BF16)
+        scale = keep.tile([P, BATCH, PACK], F32)
+        shift = keep.tile([P, BATCH, PACK], F32)
+        h_planes = [keep.tile([P, PACK, TOKENS], F32, name="h_planes%d" % b) for b in range(BATCH)]
+        a_planes = [keep.tile([P, PACK, TOKENS], BF16, name="a_planes%d" % b) for b in range(BATCH)]
+        a_grouped = [keep.tile([P, TOKENS, PACK], BF16, name="a_grouped%d" % b, align_bytes=64) for b in range(BATCH)]
+        a_codes = [keep.tile([P, TOKENS], U32, name="a_codes%d" % b, align_bytes=64) for b in range(BATCH)]
+        a_scales = [keep.tile([P, TOKENS], U8, name="a_scales%d" % b, align_bytes=64) for b in range(BATCH)]
 
-        acc_psum = ctx.enter_context(tc.psum_pool(name="acc_psum", bufs=8, reuse_waits="tile"))
+        def swish_plane(b, t):
+            nc.vector.scalar_tensor_tensor(
+                out=h_planes[b][:, t, :],
+                in0=xT[b][t // 2][:, t % 2, :],
+                scalar=scale[:, b, t : t + 1],
+                in1=posT_sb[:, t, :],
+                op0=ALU.mult,
+                op1=ALU.add,
+            )
+            nc.scalar.activation(
+                out=a_planes[b][:, t, :],
+                in_=h_planes[b][:, t, :],
+                func=ACT.Silu,
+                bias=shift[:, b, t : t + 1],
+                scale=1.0,
+            )
+
+        def regroup_a(b):
+            regroup(nc.vector.tensor_copy, a_grouped[b][:], a_planes[b][:])
+
+        def quantise_a(b):
+            nc.vector.quantize_mx(
+                out=a_codes[b][:].bitcast(FP8X4),
+                scales=a_scales[b][:],
+                in_=a_grouped[b][:].rearrange("p n t -> p (n t)"),
+            )
+
+        stats = keep.tile([P, BATCH * PACK, 6], F32)
+        mean_var = keep.tile([P, BATCH * PACK, 2], F32)
+        gains = keep.tile([P, 2 * PACK], F32)
+
+        def transpose_planes(pool, rows_sb, name):
+            banks = []
+            for h in range(PACK // 2):
+                bank = pool.tile([P, 2, TOKENS], BF16, name="%s_%d" % (name, h))
+                for t2 in range(2):
+                    t = 2 * h + t2
+                    for i in range(TOKEN_TILES):
+                        nc.tensor.transpose(bank[:, t2, i * P : (i + 1) * P], rows_sb[:, i, t * P : (t + 1) * P], ident[:])
+                banks.append(bank)
+            return banks
+
+        def statistics(b):
+            for t in range(PACK):
+                nc.vector.bn_stats(out=stats[:, b * PACK + t, :], in_=xT[b][t // 2][:, t % 2, :])
+            for t in range(PACK):
+                nc.vector.bn_aggr(out=mean_var[:, b * PACK + t, :], in_=stats[:, b * PACK + t, :])
+
+        late_psum = ctx.enter_context(tc.psum_pool(name="late_psum", bufs=1))
+        with tc.psum_pool(name="early_psum", bufs=1) as early_psum:
+            gainsT = early_psum.tile([P, 2 * TOKENS], BF16)
+            nc.tensor.transpose(gainsT[:, 0:P], gain_rows[:], ident[:])
+            nc.vector.tensor_copy(out=gains[:], in_=gainsT[:, 0 : 2 * PACK])
+
+            xT[0] = transpose_planes(early_psum, x_sb[0], "xT0")
+            statistics(0)
+            for b in range(1, BATCH):
+                xT[b] = transpose_planes(late_psum, x_sb[b], "xT%d" % b)
+                statistics(b)
+            posT = transpose_planes(early_psum, pos_sb, "posT")
+            for h in range(PACK // 2):
+                nc.scalar.copy(out=posT_sb[:, 2 * h : 2 * h + 2, :], in_=posT[h][:])
+            for c in range(PASSES_PER_STORE - 1):
+                for half in range(2):
+                    regroup_w_half(c, half, gpsimd_copy)
+
+            std = keep.tile([P, BATCH, PACK], F32)
+            rstd = keep.tile([P, BATCH, PACK], F32)
+            mean_scale = keep.tile([P, BATCH, PACK], F32)
+            mean = mean_var[:, :, 0].rearrange("p (b t) -> p b t", b=BATCH)
+            var = mean_var[:, :, 1].rearrange("p (b t) -> p b t", b=BATCH)
+            gamma = gains[:, 0:PACK].unsqueeze(1).to_broadcast([P, BATCH, PACK])
+            beta = gains[:, PACK : 2 * PACK].unsqueeze(1).to_broadcast([P, BATCH, PACK])
+            nc.scalar.activation(out=std[:], in_=var, func=ACT.Sqrt, bias=EPS, scale=1.0)
+            nc.scalar.activation(out=warm[:, 1:2], in_=std[:, 0, 0:1], func=ACT.Silu)
+            nc.vector.reciprocal(out=rstd[:], in_=std[:])
+            nc.vector.tensor_tensor(out=scale[:], in0=rstd[:], in1=gamma, op=ALU.mult)
+            nc.vector.tensor_tensor(out=mean_scale[:], in0=mean, in1=scale[:], op=ALU.mult)
+            nc.vector.tensor_tensor(out=shift[:], in0=beta, in1=mean_scale[:], op=ALU.subtract)
+
+            for t in range(PACK):
+                swish_plane(0, t)
+
+        for half in range(2):
+            regroup_w_half(PASSES_PER_STORE - 1, half, nc.scalar.copy)
+        quantise_w_chunk(0)
+        regroup_a(0)
+        for c in range(1, PASSES_PER_STORE - 1):
+            quantise_w_chunk(c)
+        quantise_a(0)
+        quantise_w_chunk(PASSES_PER_STORE - 1)
+
+        acc_psum = ctx.enter_context(tc.psum_pool(name="acc_psum", bufs=6, reuse_waits="tile"))
         for g in range(N_GROUPS):
             for u in range(UNITS):
                 b, i = divmod(u, TOKEN_TILES)
-                if g == 0 and b > 0 and i == 0:
-                    swish(b)
-                    regroup_a(b)
-                    quantise_a(b)
                 tokens = slice(i * P, (i + 1) * P)
                 result = out_stage.tile([P, GROUP], F32)
                 for j in range(PASSES_PER_STORE):
@@ -201,7 +223,7 @@ def tile_attentionblock_pa_kernel(tc, x, pos_enc, gamma1, beta1, W_qkv, b_qkv, o
                         stop=True,
                     )
                     part = result[:, j * N_PASS : (j + 1) * N_PASS]
-                    if j == 0:
+                    if ((g * UNITS + u) * PASSES_PER_STORE + j) % SCALAR_SHARE == 0:
                         nc.scalar.copy(out=part, in_=acc[:])
                         nc.gpsimd.tensor_tensor(out=part, in0=part, in1=bias_sb[:, cols], op=ALU.add)
                     else:
@@ -210,6 +232,11 @@ def tile_attentionblock_pa_kernel(tc, x, pos_enc, gamma1, beta1, W_qkv, b_qkv, o
                     out=out[b].rearrange("(m i) n -> i m n", i=TOKEN_TILES)[i, :, g * GROUP : (g + 1) * GROUP],
                     in_=result[:],
                 )
+                if g == 0 and b + 1 < BATCH:
+                    swish_plane(b + 1, i)
+                    if i == TOKEN_TILES - 1:
+                        regroup_a(b + 1)
+                        quantise_a(b + 1)
                 if g + 1 < N_GROUPS:
                     next_first = (g + 1) * PASSES_PER_STORE
                     if u < 2 * PASSES_PER_STORE:

@@ -27,8 +27,6 @@ RUN = 4
 
 FLOPS = 2 * BATCH * TOKENS * D_IN * D_OUT
 
-assert PACK == TOKEN_TILES
-
 
 def regroup(copy, grouped, planes):
     copy(
@@ -70,10 +68,11 @@ def tile_attentionblock_pa_kernel(tc, x, pos_enc, gamma1, beta1, W_qkv, b_qkv, o
 
         for b in range(BATCH):
             load_x(b)
-        load_w(0)
         nc.sync.dma_start(out=pos_sb[:], in_=pos_enc[0].rearrange("(m i) d -> m i d", i=TOKEN_TILES))
+        load_w(0)
+        load_w(1)
         nc.sync.dma_start(out=bias_sb[:], in_=b_qkv.partition_broadcast(P))
-        for g in range(1, N_GROUPS):
+        for g in range(2, N_GROUPS):
             load_w(g)
 
         w_codes = keep.tile([P, D_OUT], U32, align_bytes=64)
@@ -143,10 +142,10 @@ def tile_attentionblock_pa_kernel(tc, x, pos_enc, gamma1, beta1, W_qkv, b_qkv, o
         mean_var = keep.tile([P, BATCH * PACK, 2], F32)
         gains = keep.tile([P, 2 * PACK], F32)
 
-        def transpose_planes(pool, rows_sb, name):
+        def transpose_planes(rows_sb, name):
             banks = []
             for h in range(PACK // 2):
-                bank = pool.tile([P, 2, TOKENS], BF16, name="%s_%d" % (name, h))
+                bank = head_psum.tile([P, 2, TOKENS], BF16, name="%s_%d" % (name, h))
                 for t2 in range(2):
                     t = 2 * h + t2
                     for i in range(TOKEN_TILES):
@@ -160,23 +159,21 @@ def tile_attentionblock_pa_kernel(tc, x, pos_enc, gamma1, beta1, W_qkv, b_qkv, o
             for t in range(PACK):
                 nc.vector.bn_aggr(out=mean_var[:, b * PACK + t, :], in_=stats[:, b * PACK + t, :])
 
-        late_psum = ctx.enter_context(tc.psum_pool(name="late_psum", bufs=1))
-        with tc.psum_pool(name="early_psum", bufs=1) as early_psum:
-            gainsT = early_psum.tile([P, 2 * TOKENS], BF16)
+        with tc.psum_pool(name="head_psum", bufs=1) as head_psum:
+            gainsT = head_psum.tile([P, 2 * TOKENS], BF16)
             nc.tensor.transpose(gainsT[:, 0:P], gain_rows[:], ident[:])
             nc.vector.tensor_copy(out=gains[:], in_=gainsT[:, 0 : 2 * PACK])
 
-            xT[0] = transpose_planes(early_psum, x_sb[0], "xT0")
-            statistics(0)
-            for b in range(1, BATCH):
-                xT[b] = transpose_planes(late_psum, x_sb[b], "xT%d" % b)
+            for b in range(BATCH):
+                xT[b] = transpose_planes(x_sb[b], "xT%d" % b)
                 statistics(b)
-            posT = transpose_planes(early_psum, pos_sb, "posT")
+            posT = transpose_planes(pos_sb, "posT")
             for h in range(PACK // 2):
                 nc.scalar.copy(out=posT_sb[:, 2 * h : 2 * h + 2, :], in_=posT[h][:])
-            for c in range(PASSES_PER_STORE - 1):
-                for half in range(2):
-                    regroup_w_half(c, half, gpsimd_copy)
+            for half in range(2):
+                regroup_w_half(PASSES_PER_STORE - 1, half, gpsimd_copy)
+            for half in range(2):
+                regroup_w_half(0, half, nc.vector.tensor_copy)
 
             std = keep.tile([P, BATCH, PACK], F32)
             rstd = keep.tile([P, BATCH, PACK], F32)
@@ -192,19 +189,22 @@ def tile_attentionblock_pa_kernel(tc, x, pos_enc, gamma1, beta1, W_qkv, b_qkv, o
             nc.vector.tensor_tensor(out=mean_scale[:], in0=mean, in1=scale[:], op=ALU.mult)
             nc.vector.tensor_tensor(out=shift[:], in0=beta, in1=mean_scale[:], op=ALU.subtract)
 
-            for t in range(PACK):
-                swish_plane(0, t)
+            for b in range(BATCH):
+                for t in range(PACK):
+                    swish_plane(b, t)
+                if b == 0:
+                    for c in range(1, PASSES_PER_STORE - 1):
+                        for half in range(2):
+                            regroup_w_half(c, half, nc.scalar.copy)
 
-        for half in range(2):
-            regroup_w_half(PASSES_PER_STORE - 1, half, nc.scalar.copy)
-        quantise_w_chunk(0)
         regroup_a(0)
-        for c in range(1, PASSES_PER_STORE - 1):
-            quantise_w_chunk(c)
+        quantise_w_chunk(0)
         quantise_a(0)
         quantise_w_chunk(PASSES_PER_STORE - 1)
+        for c in range(1, PASSES_PER_STORE - 1):
+            quantise_w_chunk(c)
 
-        acc_psum = ctx.enter_context(tc.psum_pool(name="acc_psum", bufs=6, reuse_waits="tile"))
+        acc_psum = ctx.enter_context(tc.psum_pool(name="acc_psum", bufs=8, reuse_waits="tile"))
         for g in range(N_GROUPS):
             for u in range(UNITS):
                 b, i = divmod(u, TOKEN_TILES)
@@ -233,9 +233,9 @@ def tile_attentionblock_pa_kernel(tc, x, pos_enc, gamma1, beta1, W_qkv, b_qkv, o
                     in_=result[:],
                 )
                 if g == 0 and b + 1 < BATCH:
-                    swish_plane(b + 1, i)
-                    if i == TOKEN_TILES - 1:
+                    if i == 0:
                         regroup_a(b + 1)
+                    if i == 1:
                         quantise_a(b + 1)
                 if g + 1 < N_GROUPS:
                     next_first = (g + 1) * PASSES_PER_STORE

from contextlib import ExitStack

import concourse.mybir as mybir
from concourse.masks import make_identity

F32 = mybir.dt.float32
BF16 = mybir.dt.bfloat16
U32 = mybir.dt.uint32
U8 = mybir.dt.uint8
FP8X4 = mybir.dt.float8_e4m3fn_x4
ALU = mybir.AluOpType
ACT = mybir.ActivationFunctionType

P = 128
PACK = 4
BATCH, TOKENS, D_IN, D_OUT = 2, 512, 512, 6144
EPS = 1e-5
TOKEN_TILES = TOKENS // P
UNITS = BATCH * TOKEN_TILES
N_PASS = 512
HALF = N_PASS // 2
PASSES_PER_STORE = 3
GROUP = N_PASS * PASSES_PER_STORE
N_GROUPS = D_OUT // GROUP
SCALAR_SHARE = 3
RUN = 4

FLOPS = 2 * BATCH * TOKENS * D_IN * D_OUT


def regroup(copy, grouped, planes):
    copy(
        out=grouped.rearrange("p (c i) t -> p c t i", i=RUN),
        in_=planes.rearrange("p t (c i) -> p c t i", i=RUN),
    )


def tile_attentionblock_pa_kernel(tc, x, pos_enc, gamma1, beta1, W_qkv, b_qkv, out):
    nc = tc.nc
    with ExitStack() as ctx:
        ctx.enter_context(tc.manual_schedule())
        keep = ctx.enter_context(tc.tile_pool(name="keep", bufs=1))
        w_stage = ctx.enter_context(tc.tile_pool(name="w_stage", bufs=4))
        out_stage = ctx.enter_context(tc.tile_pool(name="out_stage", bufs=8))

        gain_rows = keep.tile([P, P], BF16)
        nc.vector.memset(gain_rows[:], 0.0)
        one = keep.tile([P, 1], F32)
        nc.vector.memset(one[:], 1.0)
        ident = keep.tile([P, P], BF16)
        make_identity(nc, ident[:])
        warm = keep.tile([P, 2], F32)
        nc.scalar.activation(out=warm[:, 0:1], in_=one[:], func=ACT.Sqrt)

        nc.sync.dma_start(out=gain_rows[0:PACK, :], in_=gamma1.rearrange("a b (t p) -> (a b t) p", p=P))
        nc.sync.dma_start(out=gain_rows[PACK : 2 * PACK, :], in_=beta1.rearrange("a b (t p) -> (a b t) p", p=P))
        x_sb = [keep.tile([P, TOKEN_TILES, D_IN], BF16, name="x_sb%d" % b) for b in range(BATCH)]
        pos_sb = keep.tile([P, TOKEN_TILES, D_IN], BF16)
        w_raw = [keep.tile([P, PACK, GROUP], BF16, name="w_raw%d" % g) for g in range(N_GROUPS)]
        bias_sb = keep.tile([P, D_OUT], BF16)
        w_planes = W_qkv.rearrange("(t p) n -> p t n", p=P)

        def load_x(b):
            nc.sync.dma_start(out=x_sb[b][:], in_=x[b].rearrange("(m i) d -> m i d", i=TOKEN_TILES))

        def load_w(g):
            nc.sync.dma_start(out=w_raw[g][:], in_=w_planes[:, :, g * GROUP : (g + 1) * GROUP])

        for b in range(BATCH):
            load_x(b)
        nc.sync.dma_start(out=pos_sb[:], in_=pos_enc[0].rearrange("(m i) d -> m i d", i=TOKEN_TILES))
        load_w(0)
        load_w(1)
        nc.sync.dma_start(out=bias_sb[:], in_=b_qkv.partition_broadcast(P))
        for g in range(2, N_GROUPS):
            load_w(g)

        w_codes = keep.tile([P, D_OUT], U32, align_bytes=64)
        w_scales = keep.tile([P, D_OUT], U8, align_bytes=64)
        w_grouped = {}

        def regroup_w_half(c, half, copy):
            g, j = divmod(c, PASSES_PER_STORE)
            if half == 0:
                w_grouped[c] = w_stage.tile([P, N_PASS, PACK], BF16, name="w_grouped", align_bytes=64)
            first = half * HALF
            regroup(
                copy,
                w_grouped[c][:, first : first + HALF, :],
                w_raw[g][:, :, j * N_PASS + first : j * N_PASS + first + HALF],
            )

        def gpsimd_copy(out, in_):
            nc.gpsimd.tensor_scalar(out=out, in0=in_, scalar1=1.0, scalar2=0.0, op0=ALU.mult, op1=ALU.add)

        def quantise_w_chunk(c):
            cols = slice(c * N_PASS, (c + 1) * N_PASS)
            nc.vector.quantize_mx(
                out=w_codes[:, cols].bitcast(FP8X4),
                scales=w_scales[:, cols],
                in_=w_grouped[c][:].rearrange("p n t -> p (n t)"),
            )

        xT = {}
        posT_sb = keep.tile([P, PACK, TOKENS], BF16)
        scale = keep.tile([P, BATCH, PACK], F32)
        shift = keep.tile([P, BATCH, PACK], F32)
        h_planes = [keep.tile([P, PACK, TOKENS], F32, name="h_planes%d" % b) for b in range(BATCH)]
        a_planes = [keep.tile([P, PACK, TOKENS], BF16, name="a_planes%d" % b) for b in range(BATCH)]
        a_grouped = [keep.tile([P, TOKENS, PACK], BF16, name="a_grouped%d" % b, align_bytes=64) for b in range(BATCH)]
        a_codes = [keep.tile([P, TOKENS], U32, name="a_codes%d" % b, align_bytes=64) for b in range(BATCH)]
        a_scales = [keep.tile([P, TOKENS], U8, name="a_scales%d" % b, align_bytes=64) for b in range(BATCH)]

        def swish_plane(b, t):
            nc.vector.scalar_tensor_tensor(
                out=h_planes[b][:, t, :],
                in0=xT[b][t // 2][:, t % 2, :],
                scalar=scale[:, b, t : t + 1],
                in1=posT_sb[:, t, :],
                op0=ALU.mult,
                op1=ALU.add,
            )
            nc.scalar.activation(
                out=a_planes[b][:, t, :],
                in_=h_planes[b][:, t, :],
                func=ACT.Silu,
                bias=shift[:, b, t : t + 1],
                scale=1.0,
            )

        def regroup_a(b):
            regroup(nc.vector.tensor_copy, a_grouped[b][:], a_planes[b][:])

        def quantise_a(b):
            nc.vector.quantize_mx(
                out=a_codes[b][:].bitcast(FP8X4),
                scales=a_scales[b][:],
                in_=a_grouped[b][:].rearrange("p n t -> p (n t)"),
            )

        stats = keep.tile([P, BATCH * PACK, 6], F32)
        mean_var = keep.tile([P, BATCH * PACK, 2], F32)
        gains = keep.tile([P, 2 * PACK], F32)

        def transpose_planes(rows_sb, name):
            banks = []
            for h in range(PACK // 2):
                bank = head_psum.tile([P, 2, TOKENS], BF16, name="%s_%d" % (name, h))
                for t2 in range(2):
                    t = 2 * h + t2
                    for i in range(TOKEN_TILES):
                        nc.tensor.transpose(bank[:, t2, i * P : (i + 1) * P], rows_sb[:, i, t * P : (t + 1) * P], ident[:])
                banks.append(bank)
            return banks

        def statistics(b):
            for t in range(PACK):
                nc.vector.bn_stats(out=stats[:, b * PACK + t, :], in_=xT[b][t // 2][:, t % 2, :])
            for t in range(PACK):
                nc.vector.bn_aggr(out=mean_var[:, b * PACK + t, :], in_=stats[:, b * PACK + t, :])

        with tc.psum_pool(name="head_psum", bufs=1) as head_psum:
            gainsT = head_psum.tile([P, 2 * TOKENS], BF16)
            nc.tensor.transpose(gainsT[:, 0:P], gain_rows[:], ident[:])
            nc.vector.tensor_copy(out=gains[:], in_=gainsT[:, 0 : 2 * PACK])

            for b in range(BATCH):
                xT[b] = transpose_planes(x_sb[b], "xT%d" % b)
                statistics(b)
            posT = transpose_planes(pos_sb, "posT")
            for h in range(PACK // 2):
                nc.scalar.copy(out=posT_sb[:, 2 * h : 2 * h + 2, :], in_=posT[h][:])
            for half in range(2):
                regroup_w_half(PASSES_PER_STORE - 1, half, gpsimd_copy)
            for half in range(2):
                regroup_w_half(0, half, nc.vector.tensor_copy)

            std = keep.tile([P, BATCH, PACK], F32)
            rstd = keep.tile([P, BATCH, PACK], F32)
            mean_scale = keep.tile([P, BATCH, PACK], F32)
            mean = mean_var[:, :, 0].rearrange("p (b t) -> p b t", b=BATCH)
            var = mean_var[:, :, 1].rearrange("p (b t) -> p b t", b=BATCH)
            gamma = gains[:, 0:PACK].unsqueeze(1).to_broadcast([P, BATCH, PACK])
            beta = gains[:, PACK : 2 * PACK].unsqueeze(1).to_broadcast([P, BATCH, PACK])
            nc.scalar.activation(out=std[:], in_=var, func=ACT.Sqrt, bias=EPS, scale=1.0)
            nc.scalar.activation(out=warm[:, 1:2], in_=std[:, 0, 0:1], func=ACT.Silu)
            nc.vector.reciprocal(out=rstd[:], in_=std[:])
            nc.vector.tensor_tensor(out=scale[:], in0=rstd[:], in1=gamma, op=ALU.mult)
            nc.vector.tensor_tensor(out=mean_scale[:], in0=mean, in1=scale[:], op=ALU.mult)
            nc.vector.tensor_tensor(out=shift[:], in0=beta, in1=mean_scale[:], op=ALU.subtract)

            for b in range(BATCH):
                for t in range(PACK):
                    swish_plane(b, t)
                if b == 0:
                    for c in range(1, PASSES_PER_STORE - 1):
                        for half in range(2):
                            regroup_w_half(c, half, nc.scalar.copy)

        regroup_a(0)
        quantise_w_chunk(0)
        quantise_a(0)
        quantise_w_chunk(PASSES_PER_STORE - 1)
        for c in range(1, PASSES_PER_STORE - 1):
            quantise_w_chunk(c)

        acc_psum = ctx.enter_context(tc.psum_pool(name="acc_psum", bufs=8, reuse_waits="tile"))
        for g in range(N_GROUPS):
            for u in range(UNITS):
                b, i = divmod(u, TOKEN_TILES)
                tokens = slice(i * P, (i + 1) * P)
                result = out_stage.tile([P, GROUP], F32)
                for j in range(PASSES_PER_STORE):
                    cols = slice(g * GROUP + j * N_PASS, g * GROUP + (j + 1) * N_PASS)
                    acc = acc_psum.tile([P, N_PASS], F32)
                    nc.tensor.matmul_mx(
                        out=acc[:],
                        lhsT=a_codes[b][:, tokens].bitcast(FP8X4),
                        lhsT_scale=a_scales[b][:, tokens],
                        rhs=w_codes[:, cols].bitcast(FP8X4),
                        rhs_scale=w_scales[:, cols],
                        start=True,
                        stop=True,
                    )
                    part = result[:, j * N_PASS : (j + 1) * N_PASS]
                    if ((g * UNITS + u) * PASSES_PER_STORE + j) % SCALAR_SHARE == 0:
                        nc.scalar.copy(out=part, in_=acc[:])
                        nc.gpsimd.tensor_tensor(out=part, in0=part, in1=bias_sb[:, cols], op=ALU.add)
                    else:
                        nc.vector.tensor_tensor(out=part, in0=acc[:], in1=bias_sb[:, cols], op=ALU.add)
                nc.sync.dma_start(
                    out=out[b].rearrange("(m i) n -> i m n", i=TOKEN_TILES)[i, :, g * GROUP : (g + 1) * GROUP],
                    in_=result[:],
                )
                if g == 0 and b + 1 < BATCH:
                    if i == 0:
                        regroup_a(b + 1)
                    if i == 1:
                        quantise_a(b + 1)
                if g + 1 < N_GROUPS:
                    next_first = (g + 1) * PASSES_PER_STORE
                    if u < 2 * PASSES_PER_STORE:
                        regroup_w_half(next_first + u // 2, u % 2, nc.scalar.copy)
                    if u >= 2 and u % 2 == 0:
                        quantise_w_chunk(next_first + u // 2 - 1)
